import numpy as np
import ml_dtypes

BF16 = ml_dtypes.bfloat16


def bf(x):
    return np.asarray(x, np.float32).astype(BF16)


def f32(x):
    return np.asarray(x, np.float32)


def f64(x):
    return np.asarray(x).astype(np.float64)


def striped(idx):
    return np.tile(idx.reshape(-1, 16).T, (8, 1))


S, D, D2, N, H, K = 256, 128, 256, 512, 128, 4
EPS = 1e-5


def setup_inputs():
    return {"table": bf(np.random.standard_normal((S, D))), "w_left": bf(np.random.standard_normal((D, D)) / np.sqrt(D2)), "w_right": bf(np.random.standard_normal((D, D)) / np.sqrt(D2)), "w_comb": bf(np.random.standard_normal((D2, D)) / np.sqrt(D2)), "b_comb": f32(0.3 * np.random.standard_normal((D, 1))), "w_ff": bf(np.random.standard_normal((D, D)) * np.sqrt(2.0 / D)), "norm_w": f32(1.0 + 0.1 * np.random.standard_normal((D, 1))), "norm_b": f32(0.1 * np.random.standard_normal((D, 1))), "offs": striped(np.concatenate([np.random.permutation(S)[:H] for _ in range(K)]))}


def reference(table, w_left, w_right, w_comb, b_comb, w_ff, norm_w, norm_b, offs):
    idx = offs[:16].T.reshape(-1)
    t = f64(table).T
    info = f64(w_left).T @ t[:, idx[:S]] + f64(w_right).T @ t[:, idx[S:]]
    hid = np.maximum(f64(w_comb)[:D].T @ t + f64(w_comb)[D:].T @ info + f64(b_comb), 0.0)
    added = t + f64(w_ff).T @ hid
    mean = added.mean(axis=1, keepdims=True)
    var = np.square(added - mean).mean(axis=1, keepdims=True)
    return (added - mean) / np.sqrt(var + EPS) * f64(norm_w) + f64(norm_b)

@@ -1,0 +1,92 @@
+import concourse.mybir as mybir
+from concourse.masks import make_identity
+
+P = 128
+S = 256
+N = 512
+EPS = 1e-5
+
+BF16, F32, U16 = mybir.dt.bfloat16, mybir.dt.float32, mybir.dt.uint16
+ACT = mybir.ActivationFunctionType
+ALU = mybir.AluOpType
+
+FLOPS = 2 * P * P * (N + 2 * S + S)
+
+
+def tile_messagepassinglayer_kernel(
+    tc, table, w_left, w_right, w_comb, b_comb, w_ff, norm_w, norm_b, offs, out
+):
+    nc = tc.nc
+    with (
+        tc.tile_pool(name="held", bufs=1) as held,
+        tc.psum_pool(name="psum", bufs=1) as psum,
+    ):
+        rows = held.tile([P, S // P, P], BF16, name="rows")
+        nc.sync.dma_start(rows[:], table.rearrange("(b p) d -> p b d", p=P))
+        offsets = held.tile([P, N // 16], U16, name="offsets")
+        nc.sync.dma_start(offsets[:], offs)
+
+        left = held.tile([P, P], BF16, name="left")
+        nc.scalar.dma_start(left[:], w_left)
+        right = held.tile([P, P], BF16, name="right")
+        nc.scalar.dma_start(right[:], w_right)
+        comb = held.tile([P, 2, P], BF16, name="comb")
+        nc.sync.dma_start(comb[:], w_comb.rearrange("(h k) m -> k h m", k=P))
+        feed = held.tile([P, P], BF16, name="feed")
+        nc.sync.dma_start(feed[:], w_ff)
+
+        bias = held.tile([P, 1], F32, name="bias")
+        gain = held.tile([P, 1], F32, name="gain")
+        shift = held.tile([P, 1], F32, name="shift")
+        with nc.allow_non_contiguous_dma(reason="one float32 to a partition"):
+            nc.scalar.dma_start(bias[:], b_comb)
+            nc.gpsimd.dma_start(gain[:], norm_w)
+            nc.gpsimd.dma_start(shift[:], norm_b)
+
+        identity = held.tile([P, P], BF16, name="identity")
+        make_identity(nc, identity[:])
+        eps = held.tile([P, 1], F32, name="eps")
+        nc.vector.memset(eps[:], EPS)
+
+        flipped = psum.tile([P, S], BF16, name="flipped")
+        for b in range(S // P):
+            nc.tensor.transpose(flipped[:, b * P : (b + 1) * P], rows[:, b, :], identity[:])
+        window = held.tile([P, S], BF16, name="window")
+        nc.vector.tensor_copy(window[:], flipped[:])
+
+        k = S // 16
+        info_sum = psum.tile([P, S], F32, name="info_sum")
+        nc.tensor.matmul(
+            info_sum[:], left[:], window[:].indirect(offsets[:, 0:k]), start=True, stop=False
+        )
+        nc.tensor.matmul(
+            info_sum[:], right[:], window[:].indirect(offsets[:, k : 2 * k]), start=False, stop=True
+        )
+        info = held.tile([P, S], BF16, name="info")
+        nc.vector.tensor_copy(info[:], info_sum[:])
+
+        hid_sum = psum.tile([P, S], F32, name="hid_sum")
+        nc.tensor.matmul(hid_sum[:], comb[:, 0, :], window[:], start=True, stop=False)
+        nc.tensor.matmul(hid_sum[:], comb[:, 1, :], info[:], start=False, stop=True)
+        hid = held.tile([P, S], BF16, name="hid")
+        nc.scalar.activation(hid[:], hid_sum[:], ACT.Relu, bias=bias[:])
+
+        added = psum.tile([P, S], F32, name="added")
+        nc.tensor.matmul(added[:], identity[:], window[:], start=True, stop=False)
+        nc.tensor.matmul(added[:], feed[:], hid[:], start=False, stop=True)
+
+        stats = held.tile([P, 6], F32, name="stats")
+        nc.vector.bn_stats(stats[:], added[:])
+        mean_var = held.tile([P, 2], F32, name="mean_var")
+        nc.vector.bn_aggr(mean_var[:], stats[:])
+        std = held.tile([P, 1], F32, name="std")
+        nc.scalar.activation(std[:], mean_var[:, 1:2], ACT.Sqrt, bias=eps[:])
+        rstd = held.tile([P, 1], F32, name="rstd")
+        nc.vector.reciprocal(rstd[:], std[:])
+        centred = held.tile([P, S], F32, name="centred")
+        nc.vector.tensor_scalar(
+            centred[:], added[:], mean_var[:, 0:1], gain[:], ALU.subtract, ALU.mult
+        )
+        result = held.tile([P, S], F32, name="result")
+        nc.vector.tensor_scalar(result[:], centred[:], rstd[:], shift[:], ALU.mult, ALU.add)
+        nc.sync.dma_start(out, result[:])

@@ -25,7 +25,6 @@ def tile_messagepassinglayer_kernel(
         nc.sync.dma_start(rows[:], table.rearrange("(b p) d -> p b d", p=P))
         offsets = held.tile([P, N // 16], U16, name="offsets")
         nc.sync.dma_start(offsets[:], offs)
-
         left = held.tile([P, P], BF16, name="left")
         nc.scalar.dma_start(left[:], w_left)
         right = held.tile([P, P], BF16, name="right")
@@ -33,20 +32,21 @@ def tile_messagepassinglayer_kernel(
         comb = held.tile([P, 2, P], BF16, name="comb")
         nc.sync.dma_start(comb[:], w_comb.rearrange("(h k) m -> k h m", k=P))
         feed = held.tile([P, P], BF16, name="feed")
-        nc.sync.dma_start(feed[:], w_ff)
-
+        nc.scalar.dma_start(feed[:], w_ff)
         bias = held.tile([P, 1], F32, name="bias")
         gain = held.tile([P, 1], F32, name="gain")
         shift = held.tile([P, 1], F32, name="shift")
         with nc.allow_non_contiguous_dma(reason="one float32 to a partition"):
-            nc.scalar.dma_start(bias[:], b_comb)
-            nc.gpsimd.dma_start(gain[:], norm_w)
-            nc.gpsimd.dma_start(shift[:], norm_b)
+            nc.sync.dma_start(bias[:], b_comb)
+            nc.scalar.dma_start(gain[:], norm_w)
+            nc.sync.dma_start(shift[:], norm_b)
 
         identity = held.tile([P, P], BF16, name="identity")
         make_identity(nc, identity[:])
         eps = held.tile([P, 1], F32, name="eps")
         nc.vector.memset(eps[:], EPS)
+        warm = held.tile([P, 1], F32, name="warm")
+        nc.scalar.activation(warm[:], eps[:], ACT.Sqrt)
 
         flipped = psum.tile([P, S], BF16, name="flipped")
         for b in range(S // P):

@@ -5,6 +5,8 @@ P = 128
 S = 256
 N = 512
 EPS = 1e-5
+BANK = 512
+WARM_MATMULS = 4
 
 BF16, F32, U16 = mybir.dt.bfloat16, mybir.dt.float32, mybir.dt.uint16
 ACT = mybir.ActivationFunctionType
@@ -47,6 +49,12 @@ def tile_messagepassinglayer_kernel(
         nc.vector.memset(eps[:], EPS)
         warm = held.tile([P, 1], F32, name="warm")
         nc.scalar.activation(warm[:], eps[:], ACT.Sqrt)
+
+        zeros = held.tile([P, BANK], BF16, name="zeros")
+        nc.vector.memset(zeros[:], 0.0)
+        idle_work = psum.tile([P, BANK], F32, name="idle_work")
+        for warm_step in range(WARM_MATMULS):
+            nc.tensor.matmul(idle_work[:], zeros[:, 0:P], zeros[:], start=True, stop=True)
 
         flipped = psum.tile([P, S], BF16, name="flipped")
         for b in range(S // P):

@@ -5,8 +5,8 @@ P = 128
 S = 256
 N = 512
 EPS = 1e-5
-BANK = 512
-WARM_MATMULS = 4
+C = 128
+PIECES = S // C
 
 BF16, F32, U16 = mybir.dt.bfloat16, mybir.dt.float32, mybir.dt.uint16
 ACT = mybir.ActivationFunctionType
@@ -50,51 +50,70 @@ def tile_messagepassinglayer_kernel(
         warm = held.tile([P, 1], F32, name="warm")
         nc.scalar.activation(warm[:], eps[:], ACT.Sqrt)
 
-        zeros = held.tile([P, BANK], BF16, name="zeros")
-        nc.vector.memset(zeros[:], 0.0)
-        idle_work = psum.tile([P, BANK], F32, name="idle_work")
-        for warm_step in range(WARM_MATMULS):
-            nc.tensor.matmul(idle_work[:], zeros[:, 0:P], zeros[:], start=True, stop=True)
-
         flipped = psum.tile([P, S], BF16, name="flipped")
         for b in range(S // P):
             nc.tensor.transpose(flipped[:, b * P : (b + 1) * P], rows[:, b, :], identity[:])
         window = held.tile([P, S], BF16, name="window")
         nc.vector.tensor_copy(window[:], flipped[:])
 
-        k = S // 16
-        info_sum = psum.tile([P, S], F32, name="info_sum")
-        nc.tensor.matmul(
-            info_sum[:], left[:], window[:].indirect(offsets[:, 0:k]), start=True, stop=False
-        )
-        nc.tensor.matmul(
-            info_sum[:], right[:], window[:].indirect(offsets[:, k : 2 * k]), start=False, stop=True
-        )
-        info = held.tile([P, S], BF16, name="info")
-        nc.vector.tensor_copy(info[:], info_sum[:])
+        k = C // 16
+        info_sum = [psum.tile([P, C], F32, name=f"info_sum{h}") for h in range(PIECES)]
+        hid_sum = [psum.tile([P, C], F32, name=f"hid_sum{h}") for h in range(PIECES)]
+        added = [psum.tile([P, C], F32, name=f"added{h}") for h in range(PIECES)]
+        info = [held.tile([P, C], BF16, name=f"info{h}") for h in range(PIECES)]
+        hid = [held.tile([P, C], BF16, name=f"hid{h}") for h in range(PIECES)]
 
-        hid_sum = psum.tile([P, S], F32, name="hid_sum")
-        nc.tensor.matmul(hid_sum[:], comb[:, 0, :], window[:], start=True, stop=False)
-        nc.tensor.matmul(hid_sum[:], comb[:, 1, :], info[:], start=False, stop=True)
-        hid = held.tile([P, S], BF16, name="hid")
-        nc.scalar.activation(hid[:], hid_sum[:], ACT.Relu, bias=bias[:])
+        for h in range(PIECES):
+            at_left = h * k
+            at_right = S // 16 + h * k
+            nc.tensor.matmul(
+                info_sum[h][:],
+                left[:],
+                window[:].indirect(offsets[:, at_left : at_left + k]),
+                start=True,
+                stop=False,
+            )
+            nc.tensor.matmul(
+                info_sum[h][:],
+                right[:],
+                window[:].indirect(offsets[:, at_right : at_right + k]),
+                start=False,
+                stop=True,
+            )
+        nc.scalar.copy(info[0][:], info_sum[0][:])
+        nc.vector.tensor_copy(info[1][:], info_sum[1][:])
 
-        added = psum.tile([P, S], F32, name="added")
-        nc.tensor.matmul(added[:], identity[:], window[:], start=True, stop=False)
-        nc.tensor.matmul(added[:], feed[:], hid[:], start=False, stop=True)
+        for h in range(PIECES):
+            own = window[:, h * C : (h + 1) * C]
+            nc.tensor.matmul(hid_sum[h][:], comb[:, 0, :], own, start=True, stop=False)
+            nc.tensor.matmul(added[h][:], identity[:], own, start=True, stop=False)
 
-        stats = held.tile([P, 6], F32, name="stats")
-        nc.vector.bn_stats(stats[:], added[:])
+        for h in range(PIECES):
+            nc.tensor.matmul(hid_sum[h][:], comb[:, 1, :], info[h][:], start=False, stop=True)
+        nc.scalar.activation(hid[0][:], hid_sum[0][:], ACT.Relu, bias=bias[:])
+        nc.vector.tensor_scalar(hid[1][:], hid_sum[1][:], bias[:], 0.0, ALU.add, ALU.max)
+
+        stats = held.tile([P, PIECES, 6], F32, name="stats")
+        for h in range(PIECES):
+            nc.tensor.matmul(added[h][:], feed[:], hid[h][:], start=False, stop=True)
+            nc.vector.bn_stats(stats[:, h, :], added[h][:])
+
         mean_var = held.tile([P, 2], F32, name="mean_var")
-        nc.vector.bn_aggr(mean_var[:], stats[:])
+        nc.vector.bn_aggr(mean_var[:], stats[:].rearrange("p h s -> p (h s)"))
         std = held.tile([P, 1], F32, name="std")
         nc.scalar.activation(std[:], mean_var[:, 1:2], ACT.Sqrt, bias=eps[:])
         rstd = held.tile([P, 1], F32, name="rstd")
         nc.vector.reciprocal(rstd[:], std[:])
         centred = held.tile([P, S], F32, name="centred")
-        nc.vector.tensor_scalar(
-            centred[:], added[:], mean_var[:, 0:1], gain[:], ALU.subtract, ALU.mult
-        )
+        for h in range(PIECES):
+            nc.vector.tensor_scalar(
+                centred[:, h * C : (h + 1) * C],
+                added[h][:],
+                mean_var[:, 0:1],
+                gain[:],
+                ALU.subtract,
+                ALU.mult,
+            )
         result = held.tile([P, S], F32, name="result")
         nc.vector.tensor_scalar(result[:], centred[:], rstd[:], shift[:], ALU.mult, ALU.add)
         nc.sync.dma_start(out, result[:])

@@ -5,7 +5,7 @@ P = 128
 S = 256
 N = 512
 EPS = 1e-5
-C = 128
+C = P
 PIECES = S // C
 
 BF16, F32, U16 = mybir.dt.bfloat16, mybir.dt.float32, mybir.dt.uint16
@@ -24,17 +24,18 @@ def tile_messagepassinglayer_kernel(
         tc.psum_pool(name="psum", bufs=1) as psum,
     ):
         rows = held.tile([P, S // P, P], BF16, name="rows")
-        nc.sync.dma_start(rows[:], table.rearrange("(b p) d -> p b d", p=P))
+        nc.sync.dma_start(rows[:, 0, :], table[0:P, :])
+        nc.scalar.dma_start(rows[:, 1, :], table[P:S, :])
         offsets = held.tile([P, N // 16], U16, name="offsets")
         nc.sync.dma_start(offsets[:], offs)
         left = held.tile([P, P], BF16, name="left")
         nc.scalar.dma_start(left[:], w_left)
         right = held.tile([P, P], BF16, name="right")
-        nc.scalar.dma_start(right[:], w_right)
+        nc.sync.dma_start(right[:], w_right)
         comb = held.tile([P, 2, P], BF16, name="comb")
-        nc.sync.dma_start(comb[:], w_comb.rearrange("(h k) m -> k h m", k=P))
+        nc.scalar.dma_start(comb[:], w_comb.rearrange("(h k) m -> k h m", k=P))
         feed = held.tile([P, P], BF16, name="feed")
-        nc.scalar.dma_start(feed[:], w_ff)
+        nc.sync.dma_start(feed[:], w_ff)
         bias = held.tile([P, 1], F32, name="bias")
         gain = held.tile([P, 1], F32, name="gain")
         shift = held.tile([P, 1], F32, name="shift")
@@ -48,7 +49,7 @@ def tile_messagepassinglayer_kernel(
         eps = held.tile([P, 1], F32, name="eps")
         nc.vector.memset(eps[:], EPS)
         warm = held.tile([P, 1], F32, name="warm")
-        nc.scalar.activation(warm[:], eps[:], ACT.Sqrt)
+        nc.scalar.activation(warm[:], eps[:], ACT.Abs_reciprocal_sqrt)
 
         flipped = psum.tile([P, S], BF16, name="flipped")
         for b in range(S // P):
@@ -62,6 +63,9 @@ def tile_messagepassinglayer_kernel(
         added = [psum.tile([P, C], F32, name=f"added{h}") for h in range(PIECES)]
         info = [held.tile([P, C], BF16, name=f"info{h}") for h in range(PIECES)]
         hid = [held.tile([P, C], BF16, name=f"hid{h}") for h in range(PIECES)]
+
+        for h in range(PIECES):
+            nc.tensor.matmul(added[h][:], rows[:, h, :], identity[:], start=True, stop=False)
 
         for h in range(PIECES):
             at_left = h * k
@@ -86,7 +90,6 @@ def tile_messagepassinglayer_kernel(
         for h in range(PIECES):
             own = window[:, h * C : (h + 1) * C]
             nc.tensor.matmul(hid_sum[h][:], comb[:, 0, :], own, start=True, stop=False)
-            nc.tensor.matmul(added[h][:], identity[:], own, start=True, stop=False)
 
         for h in range(PIECES):
             nc.tensor.matmul(hid_sum[h][:], comb[:, 1, :], info[h][:], start=False, stop=True)
@@ -100,10 +103,8 @@ def tile_messagepassinglayer_kernel(
 
         mean_var = held.tile([P, 2], F32, name="mean_var")
         nc.vector.bn_aggr(mean_var[:], stats[:].rearrange("p h s -> p (h s)"))
-        std = held.tile([P, 1], F32, name="std")
-        nc.scalar.activation(std[:], mean_var[:, 1:2], ACT.Sqrt, bias=eps[:])
         rstd = held.tile([P, 1], F32, name="rstd")
-        nc.vector.reciprocal(rstd[:], std[:])
+        nc.scalar.activation(rstd[:], mean_var[:, 1:2], ACT.Abs_reciprocal_sqrt, bias=eps[:])
         centred = held.tile([P, S], F32, name="centred")
         for h in range(PIECES):
             nc.vector.tensor_scalar(
@@ -114,6 +115,8 @@ def tile_messagepassinglayer_kernel(
                 ALU.subtract,
                 ALU.mult,
             )
-        result = held.tile([P, S], F32, name="result")
-        nc.vector.tensor_scalar(result[:], centred[:], rstd[:], shift[:], ALU.mult, ALU.add)
-        nc.sync.dma_start(out, result[:])
+        result = [held.tile([P, C], F32, name=f"result{h}") for h in range(PIECES)]
+        nc.scalar.activation(result[0][:], centred[:, 0:C], ACT.Identity, bias=shift[:], scale=rstd[:])
+        nc.scalar.dma_start(out[:, 0:C], result[0][:])
+        nc.vector.tensor_scalar(result[1][:], centred[:, C:S], rstd[:], shift[:], ALU.mult, ALU.add)
+        nc.sync.dma_start(out[:, C:S], result[1][:])

@@ -24,18 +24,17 @@ def tile_messagepassinglayer_kernel(
         tc.psum_pool(name="psum", bufs=1) as psum,
     ):
         rows = held.tile([P, S // P, P], BF16, name="rows")
-        nc.sync.dma_start(rows[:, 0, :], table[0:P, :])
-        nc.scalar.dma_start(rows[:, 1, :], table[P:S, :])
+        nc.sync.dma_start(rows[:], table.rearrange("(b p) d -> p b d", p=P))
         offsets = held.tile([P, N // 16], U16, name="offsets")
         nc.sync.dma_start(offsets[:], offs)
         left = held.tile([P, P], BF16, name="left")
         nc.scalar.dma_start(left[:], w_left)
         right = held.tile([P, P], BF16, name="right")
-        nc.sync.dma_start(right[:], w_right)
+        nc.scalar.dma_start(right[:], w_right)
         comb = held.tile([P, 2, P], BF16, name="comb")
-        nc.scalar.dma_start(comb[:], w_comb.rearrange("(h k) m -> k h m", k=P))
+        nc.sync.dma_start(comb[:], w_comb.rearrange("(h k) m -> k h m", k=P))
         feed = held.tile([P, P], BF16, name="feed")
-        nc.sync.dma_start(feed[:], w_ff)
+        nc.scalar.dma_start(feed[:], w_ff)
         bias = held.tile([P, 1], F32, name="bias")
         gain = held.tile([P, 1], F32, name="gain")
         shift = held.tile([P, 1], F32, name="shift")

@@ -24,17 +24,18 @@ def tile_messagepassinglayer_kernel(
         tc.psum_pool(name="psum", bufs=1) as psum,
     ):
         rows = held.tile([P, S // P, P], BF16, name="rows")
-        nc.sync.dma_start(rows[:], table.rearrange("(b p) d -> p b d", p=P))
+        nc.sync.dma_start(rows[:, 0, :], table[0:P, :])
+        nc.scalar.dma_start(rows[:, 1, :], table[P:S, :])
         offsets = held.tile([P, N // 16], U16, name="offsets")
         nc.sync.dma_start(offsets[:], offs)
         left = held.tile([P, P], BF16, name="left")
         nc.scalar.dma_start(left[:], w_left)
         right = held.tile([P, P], BF16, name="right")
-        nc.scalar.dma_start(right[:], w_right)
+        nc.sync.dma_start(right[:], w_right)
         comb = held.tile([P, 2, P], BF16, name="comb")
-        nc.sync.dma_start(comb[:], w_comb.rearrange("(h k) m -> k h m", k=P))
+        nc.scalar.dma_start(comb[:], w_comb.rearrange("(h k) m -> k h m", k=P))
         feed = held.tile([P, P], BF16, name="feed")
-        nc.scalar.dma_start(feed[:], w_ff)
+        nc.sync.dma_start(feed[:], w_ff)
         bias = held.tile([P, 1], F32, name="bias")
         gain = held.tile([P, 1], F32, name="gain")
         shift = held.tile([P, 1], F32, name="shift")
@@ -48,7 +49,7 @@ def tile_messagepassinglayer_kernel(
         eps = held.tile([P, 1], F32, name="eps")
         nc.vector.memset(eps[:], EPS)
         warm = held.tile([P, 1], F32, name="warm")
-        nc.scalar.activation(warm[:], eps[:], ACT.Abs_reciprocal_sqrt)
+        nc.scalar.activation(warm[:], eps[:], ACT.Sqrt)
 
         flipped = psum.tile([P, S], BF16, name="flipped")
         for b in range(S // P):
@@ -102,8 +103,10 @@ def tile_messagepassinglayer_kernel(
 
         mean_var = held.tile([P, 2], F32, name="mean_var")
         nc.vector.bn_aggr(mean_var[:], stats[:].rearrange("p h s -> p (h s)"))
+        std = held.tile([P, 1], F32, name="std")
+        nc.scalar.activation(std[:], mean_var[:, 1:2], ACT.Sqrt, bias=eps[:])
         rstd = held.tile([P, 1], F32, name="rstd")
-        nc.scalar.activation(rstd[:], mean_var[:, 1:2], ACT.Abs_reciprocal_sqrt, bias=eps[:])
+        nc.vector.reciprocal(rstd[:], std[:])
         centred = held.tile([P, S], F32, name="centred")
         for h in range(PIECES):
             nc.vector.tensor_scalar(
@@ -114,8 +117,6 @@ def tile_messagepassinglayer_kernel(
                 ALU.subtract,
                 ALU.mult,
             )
-        result = [held.tile([P, C], F32, name=f"result{h}") for h in range(PIECES)]
-        nc.scalar.activation(result[0][:], centred[:, 0:C], ACT.Identity, bias=shift[:], scale=rstd[:])
-        nc.scalar.dma_start(out[:, 0:C], result[0][:])
-        nc.vector.tensor_scalar(result[1][:], centred[:, C:S], rstd[:], shift[:], ALU.mult, ALU.add)
-        nc.sync.dma_start(out[:, C:S], result[1][:])
+        result = held.tile([P, S], F32, name="result")
+        nc.vector.tensor_scalar(result[:], centred[:], rstd[:], shift[:], ALU.mult, ALU.add)
+        nc.sync.dma_start(out, result[:])

@@ -4,9 +4,12 @@ from concourse.masks import make_identity
 P = 128
 S = 256
 N = 512
-EPS = 1e-5
 C = P
 PIECES = S // C
+PER_COLUMN = 16
+BN_STATS = 6
+EPS = 1e-5
+WARM_MATMULS = 12
 
 BF16, F32, U16 = mybir.dt.bfloat16, mybir.dt.float32, mybir.dt.uint16
 ACT = mybir.ActivationFunctionType
@@ -23,10 +26,10 @@ def tile_messagepassinglayer_kernel(
         tc.tile_pool(name="held", bufs=1) as held,
         tc.psum_pool(name="psum", bufs=1) as psum,
     ):
-        rows = held.tile([P, S // P, P], BF16, name="rows")
+        rows = held.tile([P, PIECES, P], BF16, name="rows")
         nc.sync.dma_start(rows[:, 0, :], table[0:P, :])
         nc.scalar.dma_start(rows[:, 1, :], table[P:S, :])
-        offsets = held.tile([P, N // 16], U16, name="offsets")
+        offsets = held.tile([P, N // PER_COLUMN], U16, name="offsets")
         nc.sync.dma_start(offsets[:], offs)
         left = held.tile([P, P], BF16, name="left")
         nc.scalar.dma_start(left[:], w_left)
@@ -44,6 +47,12 @@ def tile_messagepassinglayer_kernel(
             nc.scalar.dma_start(gain[:], norm_w)
             nc.sync.dma_start(shift[:], norm_b)
 
+        zeros = held.tile([P, C], BF16, name="zeros")
+        nc.gpsimd.memset(zeros[:], 0.0)
+        idle_work = psum.tile([P, C], F32, name="idle_work")
+        for step in range(WARM_MATMULS):
+            nc.tensor.matmul(idle_work[:], zeros[:], zeros[:], start=True, stop=True)
+
         identity = held.tile([P, P], BF16, name="identity")
         make_identity(nc, identity[:])
         eps = held.tile([P, 1], F32, name="eps")
@@ -52,12 +61,11 @@ def tile_messagepassinglayer_kernel(
         nc.scalar.activation(warm[:], eps[:], ACT.Sqrt)
 
         flipped = psum.tile([P, S], BF16, name="flipped")
-        for b in range(S // P):
-            nc.tensor.transpose(flipped[:, b * P : (b + 1) * P], rows[:, b, :], identity[:])
+        for h in range(PIECES):
+            nc.tensor.transpose(flipped[:, h * C : (h + 1) * C], rows[:, h, :], identity[:])
         window = held.tile([P, S], BF16, name="window")
         nc.vector.tensor_copy(window[:], flipped[:])
 
-        k = C // 16
         info_sum = [psum.tile([P, C], F32, name=f"info_sum{h}") for h in range(PIECES)]
         hid_sum = [psum.tile([P, C], F32, name=f"hid_sum{h}") for h in range(PIECES)]
         added = [psum.tile([P, C], F32, name=f"added{h}") for h in range(PIECES)]
@@ -67,9 +75,10 @@ def tile_messagepassinglayer_kernel(
         for h in range(PIECES):
             nc.tensor.matmul(added[h][:], rows[:, h, :], identity[:], start=True, stop=False)
 
+        k = C // PER_COLUMN
         for h in range(PIECES):
             at_left = h * k
-            at_right = S // 16 + h * k
+            at_right = S // PER_COLUMN + h * k
             nc.tensor.matmul(
                 info_sum[h][:],
                 left[:],
@@ -90,13 +99,12 @@ def tile_messagepassinglayer_kernel(
         for h in range(PIECES):
             own = window[:, h * C : (h + 1) * C]
             nc.tensor.matmul(hid_sum[h][:], comb[:, 0, :], own, start=True, stop=False)
-
         for h in range(PIECES):
             nc.tensor.matmul(hid_sum[h][:], comb[:, 1, :], info[h][:], start=False, stop=True)
         nc.scalar.activation(hid[0][:], hid_sum[0][:], ACT.Relu, bias=bias[:])
         nc.vector.tensor_scalar(hid[1][:], hid_sum[1][:], bias[:], 0.0, ALU.add, ALU.max)
 
-        stats = held.tile([P, PIECES, 6], F32, name="stats")
+        stats = held.tile([P, PIECES, BN_STATS], F32, name="stats")
         for h in range(PIECES):
             nc.tensor.matmul(added[h][:], feed[:], hid[h][:], start=False, stop=True)
             nc.vector.bn_stats(stats[:, h, :], added[h][:])
@@ -105,8 +113,6 @@ def tile_messagepassinglayer_kernel(
         nc.vector.bn_aggr(mean_var[:], stats[:].rearrange("p h s -> p (h s)"))
         std = held.tile([P, 1], F32, name="std")
         nc.scalar.activation(std[:], mean_var[:, 1:2], ACT.Sqrt, bias=eps[:])
-        rstd = held.tile([P, 1], F32, name="rstd")
-        nc.vector.reciprocal(rstd[:], std[:])
         centred = held.tile([P, S], F32, name="centred")
         for h in range(PIECES):
             nc.vector.tensor_scalar(
@@ -117,6 +123,8 @@ def tile_messagepassinglayer_kernel(
                 ALU.subtract,
                 ALU.mult,
             )
+        rstd = held.tile([P, 1], F32, name="rstd")
+        nc.vector.reciprocal(rstd[:], std[:])
         result = held.tile([P, S], F32, name="result")
         nc.vector.tensor_scalar(result[:], centred[:], rstd[:], shift[:], ALU.mult, ALU.add)
         nc.sync.dma_start(out, result[:])

@@ -32,11 +32,11 @@ def tile_messagepassinglayer_kernel(
         offsets = held.tile([P, N // PER_COLUMN], U16, name="offsets")
         nc.sync.dma_start(offsets[:], offs)
         left = held.tile([P, P], BF16, name="left")
-        nc.scalar.dma_start(left[:], w_left)
+        nc.sync.dma_start(left[:], w_left)
         right = held.tile([P, P], BF16, name="right")
         nc.sync.dma_start(right[:], w_right)
         comb = held.tile([P, 2, P], BF16, name="comb")
-        nc.scalar.dma_start(comb[:], w_comb.rearrange("(h k) m -> k h m", k=P))
+        nc.sync.dma_start(comb[:], w_comb.rearrange("(h k) m -> k h m", k=P))
         feed = held.tile([P, P], BF16, name="feed")
         nc.sync.dma_start(feed[:], w_ff)
         bias = held.tile([P, 1], F32, name="bias")
@@ -44,7 +44,7 @@ def tile_messagepassinglayer_kernel(
         shift = held.tile([P, 1], F32, name="shift")
         with nc.allow_non_contiguous_dma(reason="one float32 to a partition"):
             nc.sync.dma_start(bias[:], b_comb)
-            nc.scalar.dma_start(gain[:], norm_w)
+            nc.sync.dma_start(gain[:], norm_w)
             nc.sync.dma_start(shift[:], norm_b)
 
         zeros = held.tile([P, C], BF16, name="zeros")

@@ -9,7 +9,6 @@ PIECES = S // C
 PER_COLUMN = 16
 BN_STATS = 6
 EPS = 1e-5
-WARM_MATMULS = 12
 
 BF16, F32, U16 = mybir.dt.bfloat16, mybir.dt.float32, mybir.dt.uint16
 ACT = mybir.ActivationFunctionType
@@ -46,12 +45,6 @@ def tile_messagepassinglayer_kernel(
             nc.sync.dma_start(bias[:], b_comb)
             nc.sync.dma_start(gain[:], norm_w)
             nc.sync.dma_start(shift[:], norm_b)
-
-        zeros = held.tile([P, C], BF16, name="zeros")
-        nc.gpsimd.memset(zeros[:], 0.0)
-        idle_work = psum.tile([P, C], F32, name="idle_work")
-        for step in range(WARM_MATMULS):
-            nc.tensor.matmul(idle_work[:], zeros[:], zeros[:], start=True, stop=True)
 
         identity = held.tile([P, P], BF16, name="identity")
         make_identity(nc, identity[:])

import concourse.mybir as mybir
from concourse.masks import make_identity

P = 128
S = 256
N = 512
C = P
PIECES = S // C
PER_COLUMN = 16
BN_STATS = 6
EPS = 1e-5

BF16, F32, U16 = mybir.dt.bfloat16, mybir.dt.float32, mybir.dt.uint16
ACT = mybir.ActivationFunctionType
ALU = mybir.AluOpType

FLOPS = 2 * P * P * (N + 2 * S + S)


def tile_messagepassinglayer_kernel(
    tc, table, w_left, w_right, w_comb, b_comb, w_ff, norm_w, norm_b, offs, out
):
    nc = tc.nc
    with (
        tc.tile_pool(name="held", bufs=1) as held,
        tc.psum_pool(name="psum", bufs=1) as psum,
    ):
        rows = held.tile([P, PIECES, P], BF16, name="rows")
        nc.sync.dma_start(rows[:, 0, :], table[0:P, :])
        nc.scalar.dma_start(rows[:, 1, :], table[P:S, :])
        offsets = held.tile([P, N // PER_COLUMN], U16, name="offsets")
        nc.sync.dma_start(offsets[:], offs)
        left = held.tile([P, P], BF16, name="left")
        nc.sync.dma_start(left[:], w_left)
        right = held.tile([P, P], BF16, name="right")
        nc.sync.dma_start(right[:], w_right)
        comb = held.tile([P, 2, P], BF16, name="comb")
        nc.sync.dma_start(comb[:], w_comb.rearrange("(h k) m -> k h m", k=P))
        feed = held.tile([P, P], BF16, name="feed")
        nc.sync.dma_start(feed[:], w_ff)
        bias = held.tile([P, 1], F32, name="bias")
        gain = held.tile([P, 1], F32, name="gain")
        shift = held.tile([P, 1], F32, name="shift")
        with nc.allow_non_contiguous_dma(reason="one float32 to a partition"):
            nc.sync.dma_start(bias[:], b_comb)
            nc.sync.dma_start(gain[:], norm_w)
            nc.sync.dma_start(shift[:], norm_b)

        identity = held.tile([P, P], BF16, name="identity")
        make_identity(nc, identity[:])
        eps = held.tile([P, 1], F32, name="eps")
        nc.vector.memset(eps[:], EPS)
        warm = held.tile([P, 1], F32, name="warm")
        nc.scalar.activation(warm[:], eps[:], ACT.Sqrt)

        flipped = psum.tile([P, S], BF16, name="flipped")
        for h in range(PIECES):
            nc.tensor.transpose(flipped[:, h * C : (h + 1) * C], rows[:, h, :], identity[:])
        window = held.tile([P, S], BF16, name="window")
        nc.vector.tensor_copy(window[:], flipped[:])

        info_sum = [psum.tile([P, C], F32, name=f"info_sum{h}") for h in range(PIECES)]
        hid_sum = [psum.tile([P, C], F32, name=f"hid_sum{h}") for h in range(PIECES)]
        added = [psum.tile([P, C], F32, name=f"added{h}") for h in range(PIECES)]
        info = [held.tile([P, C], BF16, name=f"info{h}") for h in range(PIECES)]
        hid = [held.tile([P, C], BF16, name=f"hid{h}") for h in range(PIECES)]

        for h in range(PIECES):
            nc.tensor.matmul(added[h][:], rows[:, h, :], identity[:], start=True, stop=False)

        k = C // PER_COLUMN
        for h in range(PIECES):
            at_left = h * k
            at_right = S // PER_COLUMN + h * k
            nc.tensor.matmul(
                info_sum[h][:],
                left[:],
                window[:].indirect(offsets[:, at_left : at_left + k]),
                start=True,
                stop=False,
            )
            nc.tensor.matmul(
                info_sum[h][:],
                right[:],
                window[:].indirect(offsets[:, at_right : at_right + k]),
                start=False,
                stop=True,
            )
        nc.scalar.copy(info[0][:], info_sum[0][:])
        nc.vector.tensor_copy(info[1][:], info_sum[1][:])

        for h in range(PIECES):
            own = window[:, h * C : (h + 1) * C]
            nc.tensor.matmul(hid_sum[h][:], comb[:, 0, :], own, start=True, stop=False)
        for h in range(PIECES):
            nc.tensor.matmul(hid_sum[h][:], comb[:, 1, :], info[h][:], start=False, stop=True)
        nc.scalar.activation(hid[0][:], hid_sum[0][:], ACT.Relu, bias=bias[:])
        nc.vector.tensor_scalar(hid[1][:], hid_sum[1][:], bias[:], 0.0, ALU.add, ALU.max)

        stats = held.tile([P, PIECES, BN_STATS], F32, name="stats")
        for h in range(PIECES):
            nc.tensor.matmul(added[h][:], feed[:], hid[h][:], start=False, stop=True)
            nc.vector.bn_stats(stats[:, h, :], added[h][:])

        mean_var = held.tile([P, 2], F32, name="mean_var")
        nc.vector.bn_aggr(mean_var[:], stats[:].rearrange("p h s -> p (h s)"))
        std = held.tile([P, 1], F32, name="std")
        nc.scalar.activation(std[:], mean_var[:, 1:2], ACT.Sqrt, bias=eps[:])
        centred = held.tile([P, S], F32, name="centred")
        for h in range(PIECES):
            nc.vector.tensor_scalar(
                centred[:, h * C : (h + 1) * C],
                added[h][:],
                mean_var[:, 0:1],
                gain[:],
                ALU.subtract,
                ALU.mult,
            )
        rstd = held.tile([P, 1], F32, name="rstd")
        nc.vector.reciprocal(rstd[:], std[:])
        result = held.tile([P, S], F32, name="result")
        nc.vector.tensor_scalar(result[:], centred[:], rstd[:], shift[:], ALU.mult, ALU.add)
        nc.sync.dma_start(out, result[:])
